import numpy as np
import ml_dtypes


def mxq(x, axis, fmt="e4m3"):
    dtype, down = {"e4m3": (ml_dtypes.float8_e4m3fn, 7), "e5m2": (ml_dtypes.float8_e5m2, 14)}[fmt]
    v = np.moveaxis(np.asarray(x, np.float32).astype(ml_dtypes.bfloat16).astype(np.float64), axis, -1)
    blocks = v.reshape(v.shape[:-1] + (-1, 32))
    amax = np.abs(blocks).max(-1, keepdims=True)
    byte = np.maximum(np.where(amax > 0, np.frexp(amax)[1] - 1 + 127, 0) - down, 1)
    scale = np.exp2(byte - 127.0)
    codes = (blocks / scale).astype(np.float32).astype(dtype).astype(np.float64)
    return np.moveaxis((codes * scale).reshape(v.shape), -1, axis)


WIDE = False


def mx_kscale(k):
    if not WIDE:
        return np.ones(k)
    levels = np.array([10, -10, 5, -5, 0])
    a = np.random.permutation(np.resize(levels, k // 512 * 4)).reshape(k // 512, 4)
    idx = np.arange(k)
    return np.exp2(a[idx // 512, idx % 128 // 32])


BF16 = ml_dtypes.bfloat16


def bf(x):
    return np.asarray(x, np.float32).astype(BF16)


def f64(x):
    return np.asarray(x).astype(np.float64)


B, N, F, FO, KC = 32, 512, 128, 1024, 5


def setup_inputs():
    d = mx_kscale(N)
    d = d / d.max()
    a = np.random.standard_normal((N, N)) / np.sqrt(N)
    return {"z0": bf(np.random.standard_normal((B, N, F)) * d[:, None]),
            "z1": bf(0.7 * np.random.standard_normal((B, N, F)) * d[:, None]),
            "L": bf(0.5 * (a + a.T) * d[:, None] / d[None, :])}


def reference(z0, z1, L):
    z0, z1 = f64(z0), f64(z1)
    lq = mxq(f64(L), 1, "e4m3")
    z2 = 2.0 * (lq @ mxq(z1, 1, "e4m3")) - z0
    z3 = 2.0 * (lq @ mxq(z2, 1, "e4m3")) - z1
    return z2, z3

@@ -1,0 +1,137 @@
+from contextlib import ExitStack
+
+import concourse.mybir as mybir
+from concourse.masks import make_identity
+
+FP8X4 = mybir.dt.float8_e4m3fn_x4
+BF16 = mybir.dt.bfloat16
+F32 = mybir.dt.float32
+U32 = mybir.dt.uint32
+U8 = mybir.dt.uint8
+MULT = mybir.AluOpType.mult
+SUBTRACT = mybir.AluOpType.subtract
+
+P = 128
+PACK = 4
+BATCH, NODES, FEAT = 32, 512, 128
+GROUP = 4
+COLS = GROUP * FEAT
+N_GROUPS = BATCH // GROUP
+OUT_BUFS = 8
+
+FLOPS = 2 * 2 * BATCH * NODES * NODES * FEAT
+
+assert NODES == P * PACK
+
+
+def tile_manualchebconv_pb_t_kernel(tc, z0, z1, L, out_0, out_1):
+    nc = tc.nc
+
+    def four_nodes_a_partition(dram, g):
+        return dram[g * GROUP : (g + 1) * GROUP].rearrange("b (p j) f -> p b (j f)", j=PACK)
+
+    with ExitStack() as ctx:
+        const = ctx.enter_context(tc.tile_pool(name="const", bufs=1))
+        inputs = ctx.enter_context(tc.tile_pool(name="inputs", bufs=1))
+        work = ctx.enter_context(tc.tile_pool(name="work", bufs=4))
+        results = ctx.enter_context(tc.tile_pool(name="results", bufs=OUT_BUFS))
+        psum = ctx.enter_context(tc.psum_pool(name="psum", bufs=8))
+        ctx.enter_context(tc.manual_schedule())
+
+        l_rows = const.tile([P, PACK * NODES], BF16)
+        nc.sync.dma_start(out=l_rows[:], in_=L.rearrange("(q j) m -> q (j m)", j=PACK))
+        z0_sb = []
+        z1_sb = []
+        for g in range(N_GROUPS):
+            z1_g = inputs.tile([P, GROUP, PACK, FEAT], BF16, name="z1_%d" % g)
+            nc.sync.dma_start(
+                out=z1_g[:].rearrange("p b j f -> p b (j f)"), in_=four_nodes_a_partition(z1, g)
+            )
+            z1_sb.append(z1_g)
+            z0_g = inputs.tile([P, GROUP, PACK, FEAT], BF16, name="z0_%d" % g)
+            nc.sync.dma_start(
+                out=z0_g[:].rearrange("p b j f -> p b (j f)"), in_=four_nodes_a_partition(z0, g)
+            )
+            z0_sb.append(z0_g)
+
+        identity = const.tile([P, P], F32)
+        make_identity(nc, identity[:])
+        l_words = l_rows[:].bitcast(F32).rearrange("q (j p u) -> q j u p", j=PACK, u=2)
+        l_grouped = const.tile([P, PACK * P * PACK], BF16, align_bytes=64)
+        l_grouped_words = l_grouped[:].bitcast(F32).rearrange("p (j q u) -> p j q u", j=PACK, u=2)
+        for half in range(2):
+            flipped = psum.tile([P, 2, 2, P], F32, tag="bank")
+            for jj in range(2):
+                for u in range(2):
+                    nc.tensor.transpose(
+                        flipped[:, jj, u, :], l_words[:, 2 * half + jj, u, :], identity[:]
+                    )
+            nc.vector.tensor_copy(
+                out=l_grouped_words[:, 2 * half : 2 * half + 2, :, :],
+                in_=flipped[:].rearrange("p j u q -> p j q u"),
+            )
+        l_codes = const.tile([P, PACK * P], U32, align_bytes=64)
+        l_scales = const.tile([P, PACK * P], U8, align_bytes=64)
+        nc.vector.quantize_mx(out=l_codes[:].bitcast(FP8X4), scales=l_scales[:], in_=l_grouped[:])
+
+        def regroup(z_g):
+            grouped = work.tile([P, GROUP, FEAT, PACK], BF16, align_bytes=64)
+            nc.scalar.copy(out=grouped[:], in_=z_g[:].rearrange("p b j f -> p b f j"))
+            return grouped
+
+        def quantise(grouped):
+            codes = work.tile([P, COLS], U32, align_bytes=64)
+            scales = work.tile([P, COLS], U8, align_bytes=64)
+            nc.vector.quantize_mx(
+                out=codes[:].bitcast(FP8X4),
+                scales=scales[:],
+                in_=grouped[:].rearrange("p b f j -> p (b f j)"),
+            )
+            return codes, scales
+
+        def multiply_by_l(codes, scales):
+            sums = []
+            for j in range(PACK):
+                bank = psum.tile([P, COLS], F32, tag="bank")
+                nc.tensor.matmul_mx(
+                    out=bank[:],
+                    lhsT=l_codes[:, j * P : (j + 1) * P].bitcast(FP8X4),
+                    lhsT_scale=l_scales[:, j * P : (j + 1) * P],
+                    rhs=codes[:].bitcast(FP8X4),
+                    rhs_scale=scales[:],
+                    start=True,
+                    stop=True,
+                )
+                sums.append(bank)
+            return sums
+
+        def step(sums, older, dram, g):
+            newer = results.tile([P, GROUP, PACK, FEAT], F32)
+            for j in range(PACK):
+                nc.vector.scalar_tensor_tensor(
+                    out=newer[:, :, j, :],
+                    in0=sums[j][:].rearrange("p (b f) -> p b f", b=GROUP),
+                    scalar=2.0,
+                    in1=older[:, :, j, :],
+                    op0=MULT,
+                    op1=SUBTRACT,
+                )
+            nc.sync.dma_start(
+                out=four_nodes_a_partition(dram, g), in_=newer[:].rearrange("p b j f -> p b (j f)")
+            )
+            return newer
+
+        z1_grouped = {0: regroup(z1_sb[0])}
+        z2_grouped = {}
+        for i in range(N_GROUPS + 1):
+            if i + 1 < N_GROUPS:
+                z1_grouped[i + 1] = regroup(z1_sb[i + 1])
+            if i < N_GROUPS:
+                first_sums = multiply_by_l(*quantise(z1_grouped[i]))
+            if i >= 1:
+                second_sums = multiply_by_l(*quantise(z2_grouped[i - 1]))
+            if i < N_GROUPS:
+                z2_g = step(first_sums, z0_sb[i], out_0, i)
+                z2_grouped[i] = regroup(z2_g)
+            if i >= 1:
+                step(second_sums, z1_sb[i - 1], out_1, i - 1)

@@ -121,17 +121,22 @@ def tile_manualchebconv_pb_t_kernel(tc, z0, z1, L, out_0, out_1):
             )
             return newer
 
-        z1_grouped = {0: regroup(z1_sb[0])}
+        z1_grouped = {0: regroup(z1_sb[0]), 1: regroup(z1_sb[1])}
+        first_sums = {0: multiply_by_l(*quantise(z1_grouped[0]))}
         z2_grouped = {}
-        for i in range(N_GROUPS + 1):
-            if i + 1 < N_GROUPS:
-                z1_grouped[i + 1] = regroup(z1_sb[i + 1])
+        z2_quantised = {}
+        second_sums = {}
+        for i in range(N_GROUPS + 2):
             if i < N_GROUPS:
-                first_sums = multiply_by_l(*quantise(z1_grouped[i]))
-            if i >= 1:
-                second_sums = multiply_by_l(*quantise(z2_grouped[i - 1]))
-            if i < N_GROUPS:
-                z2_g = step(first_sums, z0_sb[i], out_0, i)
+                z2_g = step(first_sums[i], z0_sb[i], out_0, i)
                 z2_grouped[i] = regroup(z2_g)
-            if i >= 1:
-                step(second_sums, z1_sb[i - 1], out_1, i - 1)
+            if 1 <= i <= N_GROUPS:
+                z2_quantised[i - 1] = quantise(z2_grouped[i - 1])
+            if i + 1 < N_GROUPS:
+                first_sums[i + 1] = multiply_by_l(*quantise(z1_grouped[i + 1]))
+            if i + 2 < N_GROUPS:
+                z1_grouped[i + 2] = regroup(z1_sb[i + 2])
+            if i >= 2:
+                step(second_sums[i - 2], z1_sb[i - 2], out_1, i - 2)
+            if 1 <= i <= N_GROUPS:
+                second_sums[i - 1] = multiply_by_l(*z2_quantised[i - 1])

@@ -15,6 +15,7 @@ P = 128
 PACK = 4
 BATCH, NODES, FEAT = 32, 512, 128
 GROUP = 4
+ROW = PACK * FEAT
 COLS = GROUP * FEAT
 N_GROUPS = BATCH // GROUP
 OUT_BUFS = 8
@@ -43,15 +44,11 @@ def tile_manualchebconv_pb_t_kernel(tc, z0, z1, L, out_0, out_1):
         z0_sb = []
         z1_sb = []
         for g in range(N_GROUPS):
-            z1_g = inputs.tile([P, GROUP, PACK, FEAT], BF16, name="z1_%d" % g)
-            nc.sync.dma_start(
-                out=z1_g[:].rearrange("p b j f -> p b (j f)"), in_=four_nodes_a_partition(z1, g)
-            )
+            z1_g = inputs.tile([P, GROUP, ROW], BF16, name="z1_%d" % g)
+            nc.sync.dma_start(out=z1_g[:], in_=four_nodes_a_partition(z1, g))
             z1_sb.append(z1_g)
-            z0_g = inputs.tile([P, GROUP, PACK, FEAT], BF16, name="z0_%d" % g)
-            nc.sync.dma_start(
-                out=z0_g[:].rearrange("p b j f -> p b (j f)"), in_=four_nodes_a_partition(z0, g)
-            )
+            z0_g = inputs.tile([P, GROUP, ROW], BF16, name="z0_%d" % g)
+            nc.sync.dma_start(out=z0_g[:], in_=four_nodes_a_partition(z0, g))
             z0_sb.append(z0_g)
 
         identity = const.tile([P, P], F32)
@@ -76,7 +73,7 @@ def tile_manualchebconv_pb_t_kernel(tc, z0, z1, L, out_0, out_1):
 
         def regroup(z_g):
             grouped = work.tile([P, GROUP, FEAT, PACK], BF16, align_bytes=64)
-            nc.scalar.copy(out=grouped[:], in_=z_g[:].rearrange("p b j f -> p b f j"))
+            nc.scalar.copy(out=grouped[:], in_=z_g[:].rearrange("p b (j f) -> p b f j", j=PACK))
             return grouped
 
         def quantise(grouped):
@@ -91,34 +88,39 @@ def tile_manualchebconv_pb_t_kernel(tc, z0, z1, L, out_0, out_1):
 
         def multiply_by_l(codes, scales):
             sums = []
-            for j in range(PACK):
-                bank = psum.tile([P, COLS], F32, tag="bank")
-                nc.tensor.matmul_mx(
-                    out=bank[:],
-                    lhsT=l_codes[:, j * P : (j + 1) * P].bitcast(FP8X4),
-                    lhsT_scale=l_scales[:, j * P : (j + 1) * P],
-                    rhs=codes[:].bitcast(FP8X4),
-                    rhs_scale=scales[:],
-                    start=True,
-                    stop=True,
-                )
+            for b in range(GROUP):
+                bank = psum.tile([P, ROW], F32, tag="bank")
+                for j in range(PACK):
+                    nc.tensor.matmul_mx(
+                        out=bank[:, j * FEAT : (j + 1) * FEAT],
+                        lhsT=l_codes[:, j * P : (j + 1) * P].bitcast(FP8X4),
+                        lhsT_scale=l_scales[:, j * P : (j + 1) * P],
+                        rhs=codes[:, b * FEAT : (b + 1) * FEAT].bitcast(FP8X4),
+                        rhs_scale=scales[:, b * FEAT : (b + 1) * FEAT],
+                        start=True,
+                        stop=True,
+                    )
                 sums.append(bank)
             return sums
 
-        def step(sums, older, dram, g):
-            newer = results.tile([P, GROUP, PACK, FEAT], F32)
-            for j in range(PACK):
+        def step(sums, older, dram, g, store_each_item):
+            newer = results.tile([P, GROUP, ROW], F32)
+            for b in range(GROUP):
                 nc.vector.scalar_tensor_tensor(
-                    out=newer[:, :, j, :],
-                    in0=sums[j][:].rearrange("p (b f) -> p b f", b=GROUP),
+                    out=newer[:, b, :],
+                    in0=sums[b][:],
                     scalar=2.0,
-                    in1=older[:, :, j, :],
+                    in1=older[:, b, :],
                     op0=MULT,
                     op1=SUBTRACT,
                 )
-            nc.sync.dma_start(
-                out=four_nodes_a_partition(dram, g), in_=newer[:].rearrange("p b j f -> p b (j f)")
-            )
+                if store_each_item:
+                    nc.sync.dma_start(
+                        out=dram[g * GROUP + b].rearrange("(p j) f -> p (j f)", j=PACK),
+                        in_=newer[:, b, :],
+                    )
+            if not store_each_item:
+                nc.sync.dma_start(out=four_nodes_a_partition(dram, g), in_=newer[:])
             return newer
 
         z1_grouped = {0: regroup(z1_sb[0]), 1: regroup(z1_sb[1])}
@@ -128,7 +130,7 @@ def tile_manualchebconv_pb_t_kernel(tc, z0, z1, L, out_0, out_1):
         second_sums = {}
         for i in range(N_GROUPS + 2):
             if i < N_GROUPS:
-                z2_g = step(first_sums[i], z0_sb[i], out_0, i)
+                z2_g = step(first_sums[i], z0_sb[i], out_0, i, False)
                 z2_grouped[i] = regroup(z2_g)
             if 1 <= i <= N_GROUPS:
                 z2_quantised[i - 1] = quantise(z2_grouped[i - 1])
@@ -137,6 +139,6 @@ def tile_manualchebconv_pb_t_kernel(tc, z0, z1, L, out_0, out_1):
             if i + 2 < N_GROUPS:
                 z1_grouped[i + 2] = regroup(z1_sb[i + 2])
             if i >= 2:
-                step(second_sums[i - 2], z1_sb[i - 2], out_1, i - 2)
+                step(second_sums[i - 2], z1_sb[i - 2], out_1, i - 2, i - 2 == N_GROUPS - 1)
             if 1 <= i <= N_GROUPS:
                 second_sums[i - 1] = multiply_by_l(*z2_quantised[i - 1])

@@ -10,6 +10,7 @@ U32 = mybir.dt.uint32
 U8 = mybir.dt.uint8
 MULT = mybir.AluOpType.mult
 SUBTRACT = mybir.AluOpType.subtract
+ADD = mybir.AluOpType.add
 
 P = 128
 PACK = 4
@@ -19,6 +20,8 @@ ROW = PACK * FEAT
 COLS = GROUP * FEAT
 N_GROUPS = BATCH // GROUP
 OUT_BUFS = 8
+Z1_BUFS = 1
+ON_GPSIMD = 2
 
 FLOPS = 2 * 2 * BATCH * NODES * NODES * FEAT
 
@@ -36,6 +39,8 @@ def tile_manualchebconv_pb_t_kernel(tc, z0, z1, L, out_0, out_1):
         inputs = ctx.enter_context(tc.tile_pool(name="inputs", bufs=1))
         work = ctx.enter_context(tc.tile_pool(name="work", bufs=4))
         results = ctx.enter_context(tc.tile_pool(name="results", bufs=OUT_BUFS))
+        beside = ctx.enter_context(tc.tile_pool(name="beside", bufs=2))
+        z1_work = ctx.enter_context(tc.tile_pool(name="z1_work", bufs=Z1_BUFS))
         psum = ctx.enter_context(tc.psum_pool(name="psum", bufs=8))
         ctx.enter_context(tc.manual_schedule())
 
@@ -50,6 +55,11 @@ def tile_manualchebconv_pb_t_kernel(tc, z0, z1, L, out_0, out_1):
             z0_g = inputs.tile([P, GROUP, ROW], BF16, name="z0_%d" % g)
             nc.sync.dma_start(out=z0_g[:], in_=four_nodes_a_partition(z0, g))
             z0_sb.append(z0_g)
+
+        one_column = const.tile([P, 1], F32)
+        nc.vector.memset(one_column[:], 0.0)
+        one_column_doubled = const.tile([P, 1], F32)
+        nc.scalar.mul(out=one_column_doubled[:], in_=one_column[:], mul=2.0)
 
         identity = const.tile([P, P], F32)
         make_identity(nc, identity[:])
@@ -76,6 +86,24 @@ def tile_manualchebconv_pb_t_kernel(tc, z0, z1, L, out_0, out_1):
             nc.scalar.copy(out=grouped[:], in_=z_g[:].rearrange("p b (j f) -> p b f j", j=PACK))
             return grouped
 
+        def regroup_z1_on_gpsimd(g):
+            z1_grouped = z1_work.tile([P, GROUP, FEAT, PACK], BF16, align_bytes=64)
+            nc.gpsimd.tensor_scalar(
+                out=z1_grouped[:, GROUP - ON_GPSIMD :],
+                in0=z1_sb[g][:, GROUP - ON_GPSIMD :].rearrange("p b (j f) -> p b f j", j=PACK),
+                scalar1=1.0,
+                scalar2=0.0,
+                op0=MULT,
+                op1=ADD,
+            )
+            return z1_grouped
+
+        def regroup_z1_on_scalar(g, z1_grouped):
+            nc.scalar.copy(
+                out=z1_grouped[:, : GROUP - ON_GPSIMD],
+                in_=z1_sb[g][:, : GROUP - ON_GPSIMD].rearrange("p b (j f) -> p b f j", j=PACK),
+            )
+
         def quantise(grouped):
             codes = work.tile([P, COLS], U32, align_bytes=64)
             scales = work.tile([P, COLS], U8, align_bytes=64)
@@ -86,9 +114,9 @@ def tile_manualchebconv_pb_t_kernel(tc, z0, z1, L, out_0, out_1):
             )
             return codes, scales
 
-        def multiply_by_l(codes, scales):
-            sums = []
-            for b in range(GROUP):
+        def multiply_by_l(codes, scales, order):
+            sums = {}
+            for b in order:
                 bank = psum.tile([P, ROW], F32, tag="bank")
                 for j in range(PACK):
                     nc.tensor.matmul_mx(
@@ -100,45 +128,75 @@ def tile_manualchebconv_pb_t_kernel(tc, z0, z1, L, out_0, out_1):
                         start=True,
                         stop=True,
                     )
-                sums.append(bank)
+                sums[b] = bank
             return sums
 
-        def step(sums, older, dram, g, store_each_item):
-            newer = results.tile([P, GROUP, ROW], F32)
-            for b in range(GROUP):
-                nc.vector.scalar_tensor_tensor(
-                    out=newer[:, b, :],
-                    in0=sums[b][:],
-                    scalar=2.0,
-                    in1=older[:, b, :],
-                    op0=MULT,
-                    op1=SUBTRACT,
-                )
-                if store_each_item:
-                    nc.sync.dma_start(
-                        out=dram[g * GROUP + b].rearrange("(p j) f -> p (j f)", j=PACK),
-                        in_=newer[:, b, :],
-                    )
-            if not store_each_item:
-                nc.sync.dma_start(out=four_nodes_a_partition(dram, g), in_=newer[:])
-            return newer
+        def step_on_vector(bank, older, newer, b):
+            nc.vector.scalar_tensor_tensor(
+                out=newer[:, b, :],
+                in0=bank[:],
+                scalar=2.0,
+                in1=older[:, b, :],
+                op0=MULT,
+                op1=SUBTRACT,
+            )
 
-        z1_grouped = {0: regroup(z1_sb[0]), 1: regroup(z1_sb[1])}
-        first_sums = {0: multiply_by_l(*quantise(z1_grouped[0]))}
+        def step_beside_vector(bank, older, newer, b):
+            doubled = beside.tile([P, ROW], F32)
+            nc.scalar.mul(out=doubled[:], in_=bank[:], mul=2.0)
+            nc.gpsimd.tensor_tensor(
+                out=newer[:, b, :], in0=doubled[:], in1=older[:, b, :], op=SUBTRACT
+            )
+
+        def store_group(dram, g, newer):
+            nc.sync.dma_start(out=four_nodes_a_partition(dram, g), in_=newer[:])
+
+        def store_item(dram, g, newer, b):
+            nc.sync.dma_start(
+                out=dram[g * GROUP + b].rearrange("(p j) f -> p (j f)", j=PACK), in_=newer[:, b, :]
+            )
+
+        ALL = list(range(GROUP))
+        LAST = N_GROUPS - 1
+        z1_ready = {0: regroup_z1_on_gpsimd(0)}
+        regroup_z1_on_scalar(0, z1_ready[0])
+        first_sums = {0: multiply_by_l(*quantise(z1_ready[0]), ALL)}
+        z1_ready[1] = regroup_z1_on_gpsimd(1)
+        regroup_z1_on_scalar(1, z1_ready[1])
         z2_grouped = {}
         z2_quantised = {}
         second_sums = {}
         for i in range(N_GROUPS + 2):
             if i < N_GROUPS:
-                z2_g = step(first_sums[i], z0_sb[i], out_0, i, False)
+                z2_g = results.tile([P, GROUP, ROW], F32, tag="newer")
+                for b in ALL:
+                    step_on_vector(first_sums[i][b], z0_sb[i], z2_g, b)
+                store_group(out_0, i, z2_g)
                 z2_grouped[i] = regroup(z2_g)
             if 1 <= i <= N_GROUPS:
                 z2_quantised[i - 1] = quantise(z2_grouped[i - 1])
             if i + 1 < N_GROUPS:
-                first_sums[i + 1] = multiply_by_l(*quantise(z1_grouped[i + 1]))
+                first_sums[i + 1] = multiply_by_l(*quantise(z1_ready[i + 1]), ALL)
             if i + 2 < N_GROUPS:
-                z1_grouped[i + 2] = regroup(z1_sb[i + 2])
+                z1_ready[i + 2] = regroup_z1_on_gpsimd(i + 2)
             if i >= 2:
-                step(second_sums[i - 2], z1_sb[i - 2], out_1, i - 2, i - 2 == N_GROUPS - 1)
+                g = i - 2
+                z3_g = results.tile([P, GROUP, ROW], F32, tag="newer")
+                if g < LAST:
+                    for b in ALL[:3]:
+                        step_on_vector(second_sums[g][b], z1_sb[g], z3_g, b)
+                    step_beside_vector(second_sums[g][3], z1_sb[g], z3_g, 3)
+                    store_group(out_1, g, z3_g)
+                else:
+                    step_beside_vector(second_sums[g][3], z1_sb[g], z3_g, 3)
+                    for b in ALL[:3]:
+                        step_on_vector(second_sums[g][b], z1_sb[g], z3_g, b)
+                        if b == 1:
+                            store_item(out_1, g, z3_g, 3)
+                        store_item(out_1, g, z3_g, b)
+            if i + 2 < N_GROUPS:
+                regroup_z1_on_scalar(i + 2, z1_ready[i + 2])
             if 1 <= i <= N_GROUPS:
-                second_sums[i - 1] = multiply_by_l(*z2_quantised[i - 1])
+                second_sums[i - 1] = multiply_by_l(
+                    *z2_quantised[i - 1], ALL if i - 1 < LAST else [3, 0, 1, 2]
+                )

@@ -148,8 +148,8 @@ def tile_manualchebconv_pb_t_kernel(tc, z0, z1, L, out_0, out_1):
                 out=newer[:, b, :], in0=doubled[:], in1=older[:, b, :], op=SUBTRACT
             )
 
-        def store_group(dram, g, newer):
-            nc.sync.dma_start(out=four_nodes_a_partition(dram, g), in_=newer[:])
+        def store_group(dram, g, newer, queue):
+            queue.dma_start(out=four_nodes_a_partition(dram, g), in_=newer[:])
 
         def store_item(dram, g, newer, b):
             nc.sync.dma_start(
@@ -171,8 +171,8 @@ def tile_manualchebconv_pb_t_kernel(tc, z0, z1, L, out_0, out_1):
                 z2_g = results.tile([P, GROUP, ROW], F32, tag="newer")
                 for b in ALL:
                     step_on_vector(first_sums[i][b], z0_sb[i], z2_g, b)
-                store_group(out_0, i, z2_g)
                 z2_grouped[i] = regroup(z2_g)
+                store_group(out_0, i, z2_g, nc.scalar)
             if 1 <= i <= N_GROUPS:
                 z2_quantised[i - 1] = quantise(z2_grouped[i - 1])
             if i + 1 < N_GROUPS:
@@ -186,7 +186,7 @@ def tile_manualchebconv_pb_t_kernel(tc, z0, z1, L, out_0, out_1):
                     for b in ALL[:3]:
                         step_on_vector(second_sums[g][b], z1_sb[g], z3_g, b)
                     step_beside_vector(second_sums[g][3], z1_sb[g], z3_g, 3)
-                    store_group(out_1, g, z3_g)
+                    store_group(out_1, g, z3_g, nc.sync)
                 else:
                     step_beside_vector(second_sums[g][3], z1_sb[g], z3_g, 3)
                     for b in ALL[:3]:

@@ -116,45 +116,42 @@ def tile_manualchebconv_pb_t_kernel(tc, z0, z1, L, out_0, out_1):
 
         def multiply_by_l(codes, scales, order):
             sums = {}
-            for b in order:
-                bank = psum.tile([P, ROW], F32, tag="bank")
-                for j in range(PACK):
-                    nc.tensor.matmul_mx(
-                        out=bank[:, j * FEAT : (j + 1) * FEAT],
-                        lhsT=l_codes[:, j * P : (j + 1) * P].bitcast(FP8X4),
-                        lhsT_scale=l_scales[:, j * P : (j + 1) * P],
-                        rhs=codes[:, b * FEAT : (b + 1) * FEAT].bitcast(FP8X4),
-                        rhs_scale=scales[:, b * FEAT : (b + 1) * FEAT],
-                        start=True,
-                        stop=True,
-                    )
-                sums[b] = bank
+            for j in order:
+                bank = psum.tile([P, COLS], F32, tag="bank")
+                nc.tensor.matmul_mx(
+                    out=bank[:],
+                    lhsT=l_codes[:, j * P : (j + 1) * P].bitcast(FP8X4),
+                    lhsT_scale=l_scales[:, j * P : (j + 1) * P],
+                    rhs=codes[:].bitcast(FP8X4),
+                    rhs_scale=scales[:],
+                    start=True,
+                    stop=True,
+                )
+                sums[j] = bank
             return sums
 
-        def step_on_vector(bank, older, newer, b):
+        def step_on_vector(bank, older, newer, j):
             nc.vector.scalar_tensor_tensor(
-                out=newer[:, b, :],
-                in0=bank[:],
+                out=newer[:, :, j * FEAT : (j + 1) * FEAT],
+                in0=bank[:].rearrange("p (b f) -> p b f", b=GROUP),
                 scalar=2.0,
-                in1=older[:, b, :],
+                in1=older[:, :, j * FEAT : (j + 1) * FEAT],
                 op0=MULT,
                 op1=SUBTRACT,
             )
 
-        def step_beside_vector(bank, older, newer, b):
-            doubled = beside.tile([P, ROW], F32)
+        def step_beside_vector(bank, older, newer, j):
+            doubled = beside.tile([P, COLS], F32)
             nc.scalar.mul(out=doubled[:], in_=bank[:], mul=2.0)
             nc.gpsimd.tensor_tensor(
-                out=newer[:, b, :], in0=doubled[:], in1=older[:, b, :], op=SUBTRACT
+                out=newer[:, :, j * FEAT : (j + 1) * FEAT],
+                in0=doubled[:].rearrange("p (b f) -> p b f", b=GROUP),
+                in1=older[:, :, j * FEAT : (j + 1) * FEAT],
+                op=SUBTRACT,
             )
 
         def store_group(dram, g, newer, queue):
             queue.dma_start(out=four_nodes_a_partition(dram, g), in_=newer[:])
-
-        def store_item(dram, g, newer, b):
-            nc.sync.dma_start(
-                out=dram[g * GROUP + b].rearrange("(p j) f -> p (j f)", j=PACK), in_=newer[:, b, :]
-            )
 
         ALL = list(range(GROUP))
         LAST = N_GROUPS - 1
@@ -191,9 +188,7 @@ def tile_manualchebconv_pb_t_kernel(tc, z0, z1, L, out_0, out_1):
                     step_beside_vector(second_sums[g][3], z1_sb[g], z3_g, 3)
                     for b in ALL[:3]:
                         step_on_vector(second_sums[g][b], z1_sb[g], z3_g, b)
-                        if b == 1:
-                            store_item(out_1, g, z3_g, 3)
-                        store_item(out_1, g, z3_g, b)
+                    store_group(out_1, g, z3_g, nc.sync)
             if i + 2 < N_GROUPS:
                 regroup_z1_on_scalar(i + 2, z1_ready[i + 2])
             if 1 <= i <= N_GROUPS:

@@ -20,6 +20,7 @@ ROW = PACK * FEAT
 COLS = GROUP * FEAT
 N_GROUPS = BATCH // GROUP
 OUT_BUFS = 8
+Z0_AHEAD = 3
 Z1_BUFS = 1
 ON_GPSIMD = 2
 
@@ -46,20 +47,25 @@ def tile_manualchebconv_pb_t_kernel(tc, z0, z1, L, out_0, out_1):
 
         l_rows = const.tile([P, PACK * NODES], BF16)
         nc.sync.dma_start(out=l_rows[:], in_=L.rearrange("(q j) m -> q (j m)", j=PACK))
-        z0_sb = []
-        z1_sb = []
-        for g in range(N_GROUPS):
-            z1_g = inputs.tile([P, GROUP, ROW], BF16, name="z1_%d" % g)
-            nc.sync.dma_start(out=z1_g[:], in_=four_nodes_a_partition(z1, g))
-            z1_sb.append(z1_g)
-            z0_g = inputs.tile([P, GROUP, ROW], BF16, name="z0_%d" % g)
-            nc.sync.dma_start(out=z0_g[:], in_=four_nodes_a_partition(z0, g))
-            z0_sb.append(z0_g)
-
         one_column = const.tile([P, 1], F32)
         nc.vector.memset(one_column[:], 0.0)
         one_column_doubled = const.tile([P, 1], F32)
         nc.scalar.mul(out=one_column_doubled[:], in_=one_column[:], mul=2.0)
+
+        z0_sb = []
+        z1_sb = []
+
+        def load_z0(g):
+            z0_g = inputs.tile([P, GROUP, ROW], BF16, name="z0_%d" % g)
+            nc.scalar.dma_start(out=z0_g[:], in_=four_nodes_a_partition(z0, g))
+            z0_sb.append(z0_g)
+
+        for g in range(N_GROUPS):
+            z1_g = inputs.tile([P, GROUP, ROW], BF16, name="z1_%d" % g)
+            nc.sync.dma_start(out=z1_g[:], in_=four_nodes_a_partition(z1, g))
+            z1_sb.append(z1_g)
+            if g < Z0_AHEAD:
+                load_z0(g)
 
         identity = const.tile([P, P], F32)
         make_identity(nc, identity[:])
@@ -170,6 +176,8 @@ def tile_manualchebconv_pb_t_kernel(tc, z0, z1, L, out_0, out_1):
                     step_on_vector(first_sums[i][b], z0_sb[i], z2_g, b)
                 z2_grouped[i] = regroup(z2_g)
                 store_group(out_0, i, z2_g, nc.scalar)
+                if i + Z0_AHEAD < N_GROUPS:
+                    load_z0(i + Z0_AHEAD)
             if 1 <= i <= N_GROUPS:
                 z2_quantised[i - 1] = quantise(z2_grouped[i - 1])
             if i + 1 < N_GROUPS:

from contextlib import ExitStack

import concourse.mybir as mybir
from concourse.masks import make_identity

FP8X4 = mybir.dt.float8_e4m3fn_x4
BF16 = mybir.dt.bfloat16
F32 = mybir.dt.float32
U32 = mybir.dt.uint32
U8 = mybir.dt.uint8
MULT = mybir.AluOpType.mult
SUBTRACT = mybir.AluOpType.subtract
ADD = mybir.AluOpType.add

P = 128
PACK = 4
BATCH, NODES, FEAT = 32, 512, 128
GROUP = 4
ROW = PACK * FEAT
COLS = GROUP * FEAT
N_GROUPS = BATCH // GROUP
OUT_BUFS = 8
Z0_AHEAD = 3
Z1_BUFS = 1
ON_GPSIMD = 2

FLOPS = 2 * 2 * BATCH * NODES * NODES * FEAT

assert NODES == P * PACK


def tile_manualchebconv_pb_t_kernel(tc, z0, z1, L, out_0, out_1):
    nc = tc.nc

    def four_nodes_a_partition(dram, g):
        return dram[g * GROUP : (g + 1) * GROUP].rearrange("b (p j) f -> p b (j f)", j=PACK)

    with ExitStack() as ctx:
        const = ctx.enter_context(tc.tile_pool(name="const", bufs=1))
        inputs = ctx.enter_context(tc.tile_pool(name="inputs", bufs=1))
        work = ctx.enter_context(tc.tile_pool(name="work", bufs=4))
        results = ctx.enter_context(tc.tile_pool(name="results", bufs=OUT_BUFS))
        beside = ctx.enter_context(tc.tile_pool(name="beside", bufs=2))
        z1_work = ctx.enter_context(tc.tile_pool(name="z1_work", bufs=Z1_BUFS))
        psum = ctx.enter_context(tc.psum_pool(name="psum", bufs=8))
        ctx.enter_context(tc.manual_schedule())

        l_rows = const.tile([P, PACK * NODES], BF16)
        nc.sync.dma_start(out=l_rows[:], in_=L.rearrange("(q j) m -> q (j m)", j=PACK))
        one_column = const.tile([P, 1], F32)
        nc.vector.memset(one_column[:], 0.0)
        one_column_doubled = const.tile([P, 1], F32)
        nc.scalar.mul(out=one_column_doubled[:], in_=one_column[:], mul=2.0)

        z0_sb = []
        z1_sb = []

        def load_z0(g):
            z0_g = inputs.tile([P, GROUP, ROW], BF16, name="z0_%d" % g)
            nc.scalar.dma_start(out=z0_g[:], in_=four_nodes_a_partition(z0, g))
            z0_sb.append(z0_g)

        for g in range(N_GROUPS):
            z1_g = inputs.tile([P, GROUP, ROW], BF16, name="z1_%d" % g)
            nc.sync.dma_start(out=z1_g[:], in_=four_nodes_a_partition(z1, g))
            z1_sb.append(z1_g)
            if g < Z0_AHEAD:
                load_z0(g)

        identity = const.tile([P, P], F32)
        make_identity(nc, identity[:])
        l_words = l_rows[:].bitcast(F32).rearrange("q (j p u) -> q j u p", j=PACK, u=2)
        l_grouped = const.tile([P, PACK * P * PACK], BF16, align_bytes=64)
        l_grouped_words = l_grouped[:].bitcast(F32).rearrange("p (j q u) -> p j q u", j=PACK, u=2)
        for half in range(2):
            flipped = psum.tile([P, 2, 2, P], F32, tag="bank")
            for jj in range(2):
                for u in range(2):
                    nc.tensor.transpose(
                        flipped[:, jj, u, :], l_words[:, 2 * half + jj, u, :], identity[:]
                    )
            nc.vector.tensor_copy(
                out=l_grouped_words[:, 2 * half : 2 * half + 2, :, :],
                in_=flipped[:].rearrange("p j u q -> p j q u"),
            )
        l_codes = const.tile([P, PACK * P], U32, align_bytes=64)
        l_scales = const.tile([P, PACK * P], U8, align_bytes=64)
        nc.vector.quantize_mx(out=l_codes[:].bitcast(FP8X4), scales=l_scales[:], in_=l_grouped[:])

        def regroup(z_g):
            grouped = work.tile([P, GROUP, FEAT, PACK], BF16, align_bytes=64)
            nc.scalar.copy(out=grouped[:], in_=z_g[:].rearrange("p b (j f) -> p b f j", j=PACK))
            return grouped

        def regroup_z1_on_gpsimd(g):
            z1_grouped = z1_work.tile([P, GROUP, FEAT, PACK], BF16, align_bytes=64)
            nc.gpsimd.tensor_scalar(
                out=z1_grouped[:, GROUP - ON_GPSIMD :],
                in0=z1_sb[g][:, GROUP - ON_GPSIMD :].rearrange("p b (j f) -> p b f j", j=PACK),
                scalar1=1.0,
                scalar2=0.0,
                op0=MULT,
                op1=ADD,
            )
            return z1_grouped

        def regroup_z1_on_scalar(g, z1_grouped):
            nc.scalar.copy(
                out=z1_grouped[:, : GROUP - ON_GPSIMD],
                in_=z1_sb[g][:, : GROUP - ON_GPSIMD].rearrange("p b (j f) -> p b f j", j=PACK),
            )

        def quantise(grouped):
            codes = work.tile([P, COLS], U32, align_bytes=64)
            scales = work.tile([P, COLS], U8, align_bytes=64)
            nc.vector.quantize_mx(
                out=codes[:].bitcast(FP8X4),
                scales=scales[:],
                in_=grouped[:].rearrange("p b f j -> p (b f j)"),
            )
            return codes, scales

        def multiply_by_l(codes, scales, order):
            sums = {}
            for j in order:
                bank = psum.tile([P, COLS], F32, tag="bank")
                nc.tensor.matmul_mx(
                    out=bank[:],
                    lhsT=l_codes[:, j * P : (j + 1) * P].bitcast(FP8X4),
                    lhsT_scale=l_scales[:, j * P : (j + 1) * P],
                    rhs=codes[:].bitcast(FP8X4),
                    rhs_scale=scales[:],
                    start=True,
                    stop=True,
                )
                sums[j] = bank
            return sums

        def step_on_vector(bank, older, newer, j):
            nc.vector.scalar_tensor_tensor(
                out=newer[:, :, j * FEAT : (j + 1) * FEAT],
                in0=bank[:].rearrange("p (b f) -> p b f", b=GROUP),
                scalar=2.0,
                in1=older[:, :, j * FEAT : (j + 1) * FEAT],
                op0=MULT,
                op1=SUBTRACT,
            )

        def step_beside_vector(bank, older, newer, j):
            doubled = beside.tile([P, COLS], F32)
            nc.scalar.mul(out=doubled[:], in_=bank[:], mul=2.0)
            nc.gpsimd.tensor_tensor(
                out=newer[:, :, j * FEAT : (j + 1) * FEAT],
                in0=doubled[:].rearrange("p (b f) -> p b f", b=GROUP),
                in1=older[:, :, j * FEAT : (j + 1) * FEAT],
                op=SUBTRACT,
            )

        def store_group(dram, g, newer, queue):
            queue.dma_start(out=four_nodes_a_partition(dram, g), in_=newer[:])

        ALL = list(range(GROUP))
        LAST = N_GROUPS - 1
        z1_ready = {0: regroup_z1_on_gpsimd(0)}
        regroup_z1_on_scalar(0, z1_ready[0])
        first_sums = {0: multiply_by_l(*quantise(z1_ready[0]), ALL)}
        z1_ready[1] = regroup_z1_on_gpsimd(1)
        regroup_z1_on_scalar(1, z1_ready[1])
        z2_grouped = {}
        z2_quantised = {}
        second_sums = {}
        for i in range(N_GROUPS + 2):
            if i < N_GROUPS:
                z2_g = results.tile([P, GROUP, ROW], F32, tag="newer")
                for b in ALL:
                    step_on_vector(first_sums[i][b], z0_sb[i], z2_g, b)
                z2_grouped[i] = regroup(z2_g)
                store_group(out_0, i, z2_g, nc.scalar)
                if i + Z0_AHEAD < N_GROUPS:
                    load_z0(i + Z0_AHEAD)
            if 1 <= i <= N_GROUPS:
                z2_quantised[i - 1] = quantise(z2_grouped[i - 1])
            if i + 1 < N_GROUPS:
                first_sums[i + 1] = multiply_by_l(*quantise(z1_ready[i + 1]), ALL)
            if i + 2 < N_GROUPS:
                z1_ready[i + 2] = regroup_z1_on_gpsimd(i + 2)
            if i >= 2:
                g = i - 2
                z3_g = results.tile([P, GROUP, ROW], F32, tag="newer")
                if g < LAST:
                    for b in ALL[:3]:
                        step_on_vector(second_sums[g][b], z1_sb[g], z3_g, b)
                    step_beside_vector(second_sums[g][3], z1_sb[g], z3_g, 3)
                    store_group(out_1, g, z3_g, nc.sync)
                else:
                    step_beside_vector(second_sums[g][3], z1_sb[g], z3_g, 3)
                    for b in ALL[:3]:
                        step_on_vector(second_sums[g][b], z1_sb[g], z3_g, b)
                    store_group(out_1, g, z3_g, nc.sync)
            if i + 2 < N_GROUPS:
                regroup_z1_on_scalar(i + 2, z1_ready[i + 2])
            if 1 <= i <= N_GROUPS:
                second_sums[i - 1] = multiply_by_l(
                    *z2_quantised[i - 1], ALL if i - 1 < LAST else [3, 0, 1, 2]
                )
